import numpy as np
import ml_dtypes


def mxq(x, axis, fmt="e4m3"):
    dtype, down = {"e4m3": (ml_dtypes.float8_e4m3fn, 7), "e5m2": (ml_dtypes.float8_e5m2, 14)}[fmt]
    v = np.moveaxis(np.asarray(x, np.float32).astype(ml_dtypes.bfloat16).astype(np.float64), axis, -1)
    blocks = v.reshape(v.shape[:-1] + (-1, 32))
    amax = np.abs(blocks).max(-1, keepdims=True)
    byte = np.maximum(np.where(amax > 0, np.frexp(amax)[1] - 1 + 127, 0) - down, 1)
    scale = np.exp2(byte - 127.0)
    codes = (blocks / scale).astype(np.float32).astype(dtype).astype(np.float64)
    return np.moveaxis((codes * scale).reshape(v.shape), -1, axis)


WIDE = False


def mx_kscale(k):
    if not WIDE:
        return np.ones(k)
    levels = np.array([10, -10, 5, -5, 0])
    a = np.random.permutation(np.resize(levels, k // 512 * 4)).reshape(k // 512, 4)
    idx = np.arange(k)
    return np.exp2(a[idx // 512, idx % 128 // 32])


BF16 = ml_dtypes.bfloat16


def bf(x):
    return np.asarray(x, np.float32).astype(BF16)


def f64(x):
    return np.asarray(x).astype(np.float64)


E2M1 = np.array([0.0, 0.5, 1.0, 1.5, 2.0, 3.0, 4.0, 6.0, -0.0, -0.5, -1.0, -1.5, -2.0, -3.0, -4.0, -6.0])


def pack_weight(w, fmt):
    k, n = w.shape
    w = f64(bf(w)).reshape(k // 32, 32, n)
    amax = np.abs(w).max(1)
    if fmt == "e4m3":
        byte = np.frexp(amax)[1] - 1 + 127 - 7
    else:
        mant, ex = np.frexp(amax / 6.0)
        byte = np.where(mant > 0.5, ex, ex - 1) + 127
    byte = np.clip(np.where(amax > 0, byte, 1), 1, 254)
    scaled = (w * np.exp2(127.0 - byte)[:, None, :]).reshape(k, n).astype(np.float32)
    by_word = np.ascontiguousarray(scaled.reshape(k // 512, 128, 4, n).transpose(0, 1, 3, 2))
    if fmt == "e4m3":
        words = by_word.astype(ml_dtypes.float8_e4m3fn).view(np.uint8)
    else:
        c = by_word.astype(ml_dtypes.float4_e2m1fn).view(np.uint8) & 0xF
        words = c[..., 0::2] | (c[..., 1::2] << 4)
    return np.ascontiguousarray(words), np.ascontiguousarray(byte.astype(np.uint8).reshape(k // 512, 16, n))


def unpack_weight(words, scales, fmt):
    g, p, n, _ = words.shape
    if fmt == "e4m3":
        vals = np.ascontiguousarray(words).view(ml_dtypes.float8_e4m3fn).astype(np.float64)
    else:
        nib = np.empty((g, p, n, 4), np.uint8)
        nib[..., 0::2] = words & 0xF
        nib[..., 1::2] = words >> 4
        vals = E2M1[nib]
    vals = vals * np.repeat(np.exp2(scales.astype(np.float64) - 127.0), 8, axis=1)[..., None]
    return vals.transpose(0, 1, 3, 2).reshape(g * 512, n)


B, S, DI, DO = 1, 128, 4096, 4096
R = B * S
LN_EPS = 1e-5
FMT = "e4m3"


def ste_sign(w):
    return np.where(w >= 0, 1.0, -1.0)


def setup_inputs():
    r = np.asarray(mx_kscale(DI), np.float64)[np.arange(R) * DI // R]
    x = bf(np.random.standard_normal((B, S, DI)) * r.reshape(B, S, 1))
    words, scales = pack_weight(ste_sign(np.random.standard_normal((DO, DI)) * 0.02).T, FMT)
    return {"x": x,
            "weight_words": words,
            "weight_scales": scales,
            "in_channel_scale": bf(np.random.uniform(0.5, 1.5, DI) / np.sqrt(DI)),
            "out_channel_scale": bf(np.random.uniform(0.5, 1.5, DO) / r.min()),
            "bias": bf(np.random.standard_normal(DO) * 0.3),
            "ln_gamma": bf(1.0 + 0.1 * np.random.standard_normal(DO)),
            "ln_beta": bf(0.1 * np.random.standard_normal(DO))}


def reference(x, weight_words, weight_scales, in_channel_scale, out_channel_scale, bias, ln_gamma, ln_beta):
    x = f64(x)
    orig_shape = x.shape
    xf = x.reshape(-1, orig_shape[-1])
    w_bin_t = unpack_weight(weight_words, weight_scales, FMT)
    xs = xf * f64(in_channel_scale)
    h = (mxq(xs, 1, "e4m3") @ w_bin_t) * f64(out_channel_scale)
    h = h + f64(bias)
    mu = np.mean(h, axis=-1, keepdims=True)
    var = np.mean(np.square(h - mu), axis=-1, keepdims=True)
    h = (h - mu) / np.sqrt(var + LN_EPS) * f64(ln_gamma) + f64(ln_beta)
    return h.reshape(*orig_shape[:-1], w_bin_t.shape[1])

@@ -1,0 +1,233 @@
+from contextlib import ExitStack
+
+import concourse.mybir as mybir
+from concourse.masks import make_identity
+
+F32 = mybir.dt.float32
+BF16 = mybir.dt.bfloat16
+I32 = mybir.dt.int32
+U32 = mybir.dt.uint32
+U8 = mybir.dt.uint8
+FP8X4 = mybir.dt.float8_e4m3fn_x4
+ALU = mybir.AluOpType
+ACT = mybir.ActivationFunctionType
+
+P = 128
+DI = 4096
+DO = 4096
+G = DI // 512
+LN_EPS = 1e-5
+FLOPS = 2 * P * DI * DO
+
+RANGES = ((0, 2048, 1), (2048, 1024, 2), (3072, 512, 4), (3584, 256, 4), (3840, 256, 2))
+
+
+def tile_onebitlinear_w_kernel(
+    tc, x, weight_words, weight_scales, in_channel_scale, out_channel_scale, bias, ln_gamma, ln_beta, out
+):
+    nc = tc.nc
+    xf = x.flatten_outer_dims()
+    of = out.flatten_outer_dims()
+    w_view = weight_words.rearrange("g p n t -> p g (n t)")
+
+    with ExitStack() as ctx:
+        const = ctx.enter_context(tc.tile_pool(name="const", bufs=1))
+        wpool = ctx.enter_context(tc.tile_pool(name="wpool", bufs=12))
+        work = ctx.enter_context(tc.tile_pool(name="work", bufs=3))
+        psum = ctx.enter_context(tc.psum_pool(name="psum", bufs=8))
+        ctx.enter_context(tc.manual_schedule())
+
+        eps = const.tile([P, 1], F32)
+        dummy = const.tile([P, 1], F32)
+        ics_rows = const.tile([P, 512], BF16)
+        vrow = const.tile([P, 256], BF16)
+        planes = const.tile([P, 2, DO], U8, align_bytes=64)
+        vmat = const.tile([P, DO], BF16)
+        cmat = const.tile([P, P], BF16)
+        ident_f = const.tile([P, P], F32)
+        ident_b = const.tile([P, P], BF16)
+        x_sb = const.tile([P, DI], BF16)
+        grouped = const.tile([P, DI], BF16, align_bytes=64)
+        xcodes = const.tile([P, DI // 4], U32, align_bytes=64)
+        xscales = const.tile([P, DI // 4], U8, align_bytes=64)
+        vcol = const.tile([P, P], F32)
+        ics_t = const.tile([P, 2 * G], F32)
+        ocs_bc = const.tile([P, DO], BF16)
+        bias_bc = const.tile([P, DO], BF16)
+        gamma_bc = const.tile([P, DO], BF16)
+        hg = const.tile([P, DO], F32)
+        n_chunks = sum(max(1, w // 512) for (n0, w, gpd) in RANGES)
+        stats = const.tile([P, n_chunks, 6], F32)
+        mv = const.tile([P, 2], F32)
+        std = const.tile([P, 1], F32)
+        rstd = const.tile([P, 1], F32)
+        c32 = const.tile([P, 1], F32)
+        r1 = const.tile([P, 1], F32)
+        lt = const.tile([P, P], BF16)
+
+        nc.sync.dma_start(out=x_sb[:], in_=xf)
+
+        nc.vector.memset(eps[:], LN_EPS)
+        nc.vector.memset(ics_rows[:].bitcast(I32), 0)
+        nc.vector.memset(vrow[:].bitcast(I32), 0)
+        nc.vector.memset(planes[:].rearrange("p a n -> p (a n)").bitcast(I32), 0)
+        nc.vector.memset(vmat[:].bitcast(I32), 0)
+        nc.vector.memset(cmat[:].bitcast(I32), 0)
+        nc.vector.memset(cmat[:, 3:4], 1.0)
+
+        make_identity(nc, ident_f[:])
+        make_identity(nc, ident_b[:])
+
+        nc.scalar.dma_start(out=ics_rows[0:G, :], in_=in_channel_scale.rearrange("(g c) -> g c", g=G))
+        nc.scalar.dma_start(out=vrow[0:16, :], in_=out_channel_scale.rearrange("(j c) -> j c", j=16))
+        nc.scalar.dma_start(out=vrow[16:32, :], in_=bias.rearrange("(j c) -> j c", j=16))
+        nc.scalar.dma_start(out=vrow[32:48, :], in_=ln_gamma.rearrange("(j c) -> j c", j=16))
+        nc.scalar.activation(out=dummy[:], in_=eps[:], func=ACT.Sqrt)
+        nc.scalar.dma_start(out=vmat[0:3, :], in_=ln_gamma.partition_broadcast(3))
+        nc.scalar.dma_start(out=vmat[3:4, :], in_=ln_beta.rearrange("(o n) -> o n", o=1))
+
+        for a in range(2):
+            for q in range(4):
+                nc.sync.dma_start(
+                    out=planes[32 * q : 32 * q + 16, a, :].bitcast(I32),
+                    in_=weight_scales[4 * a : 4 * a + 4, 4 * q : 4 * q + 4, :].bitcast(I32),
+                )
+
+        pv = psum.tile([P, P], F32, name="pv", tag="bank")
+        nc.tensor.transpose(pv[:], vrow[:].bitcast(F32), ident_f[:])
+        nc.scalar.copy(out=vcol[:], in_=pv[:])
+        pi = psum.tile([P, 2, P], F32, name="pi", tag="bank")
+        ics_words = ics_rows[:].bitcast(F32)
+        for u in range(2):
+            nc.tensor.transpose(pi[:, u, :], ics_words[:, u : 256 : 2], ident_f[:])
+        nc.scalar.copy(
+            out=ics_t[:].rearrange("p (g u) -> p g u", u=2), in_=pi[:, :, 0:G].rearrange("p u g -> p g u")
+        )
+
+        def spread(v, dst):
+            dst_words = dst[:].bitcast(F32)
+            for c in range(4):
+                pb = psum.tile([P, 512], F32, name="pb", tag="bank")
+                for i in range(4):
+                    col = 16 * v + 4 * c + i
+                    nc.tensor.transpose(
+                        pb[:, P * i : P * (i + 1)], vcol[:, col : col + 1].to_broadcast([P, P]), ident_f[:]
+                    )
+                nc.scalar.copy(out=dst_words[:, 512 * c : 512 * (c + 1)], in_=pb[:])
+
+        spread(0, ocs_bc)
+
+        x_words = x_sb[:].bitcast(F32)
+        ics_bf = ics_t[:].bitcast(BF16)
+        xts = []
+        for b in range(G // 2):
+            xt = psum.tile([P, 512], F32, name="xt", tag="bank")
+            xts.append(xt)
+            for h in range(2):
+                g = 2 * b + h
+                for u in range(2):
+                    nc.tensor.transpose(
+                        xt[:, 256 * h + P * u : 256 * h + P * (u + 1)],
+                        x_words[:, 256 * g + u : 256 * (g + 1) : 2],
+                        ident_f[:],
+                    )
+
+        def scale_x(g):
+            src = xts[g // 2][:].bitcast(BF16)[:, 512 * (g % 2) : 512 * (g % 2 + 1)]
+            nc.vector.tensor_tensor(
+                out=grouped[:, 512 * g : 512 * (g + 1)].rearrange("p (r u e) -> p r u e", u=2, e=2),
+                in0=src.rearrange("p (u r e) -> p r u e", u=2, e=2),
+                in1=ics_bf[:, 4 * g : 4 * g + 4]
+                .rearrange("p (u e) -> p u e", u=2)
+                .unsqueeze(1)
+                .to_broadcast([P, P, 2, 2]),
+                op=ALU.mult,
+            )
+
+        def quantise_x(half):
+            nc.vector.quantize_mx(
+                out=xcodes[:, 512 * half : 512 * (half + 1)].bitcast(FP8X4),
+                scales=xscales[:, 512 * half : 512 * (half + 1)],
+                in_=grouped[:, 2048 * half : 2048 * (half + 1)],
+            )
+
+        for g in range(6):
+            scale_x(g)
+        quantise_x(0)
+        scale_x(6)
+        scale_x(7)
+        quantise_x(1)
+
+        spread(1, bias_bc)
+        spread(2, gamma_bc)
+
+        def to_h(acc, n0, width, chunk):
+            cols = slice(n0, n0 + width)
+            t1 = work.tile([P, 512], F32, name="t1", tag="t1")
+            h = work.tile([P, 512], F32, name="h", tag="h")
+            nc.vector.tensor_tensor(out=t1[:, 0:width], in0=acc, in1=ocs_bc[:, cols], op=ALU.mult)
+            nc.vector.tensor_tensor(out=h[:, 0:width], in0=t1[:, 0:width], in1=bias_bc[:, cols], op=ALU.add)
+            nc.vector.bn_stats(out=stats[:, chunk, :], in_=h[:, 0:width])
+            return h
+
+        def to_hg(h, n0, width):
+            cols = slice(n0, n0 + width)
+            nc.vector.tensor_tensor(out=hg[:, cols], in0=h[:, 0:width], in1=gamma_bc[:, cols], op=ALU.mult)
+
+        chunk = 0
+        last_h = None
+        for ri, (n0, w, gpd) in enumerate(RANGES):
+            nt = min(512, w)
+            accs = []
+            for j in range(w // nt):
+                acc = psum.tile([P, nt], F32, name="acc", tag="bank")
+                accs.append(acc)
+            for g0 in range(0, G, gpd):
+                wt = wpool.tile([P, gpd, w], U32, name="wt", tag="wt", align_bytes=64)
+                nc.sync.dma_start(
+                    out=wt[:].bitcast(I32), in_=w_view[:, g0 : g0 + gpd, 4 * n0 : 4 * (n0 + w)].bitcast(I32)
+                )
+                for gi in range(gpd):
+                    g = g0 + gi
+                    for j in range(w // nt):
+                        nc.tensor.matmul_mx(
+                            out=accs[j][:],
+                            lhsT=xcodes[:, P * g : P * (g + 1)].bitcast(FP8X4),
+                            lhsT_scale=xscales[:, P * g : P * (g + 1)],
+                            rhs=wt[:, gi, nt * j : nt * (j + 1)].bitcast(FP8X4),
+                            rhs_scale=planes[4 * (g % 4) : P, g // 4, n0 + nt * j : n0 + nt * (j + 1)],
+                            start=(g == 0),
+                            stop=(g == G - 1),
+                        )
+            for j in range(w // nt):
+                h = to_h(accs[j][:], n0 + nt * j, nt, chunk)
+                chunk += 1
+                if ri == len(RANGES) - 1:
+                    last_h = h
+                else:
+                    to_hg(h, n0 + nt * j, nt)
+
+        nc.vector.bn_aggr(out=mv[:], in_=stats[:].rearrange("p c s -> p (c s)"))
+        nc.scalar.activation(out=std[:], in_=mv[:, 1:2], func=ACT.Sqrt, bias=eps[:, 0:1], scale=1.0)
+        to_hg(last_h, RANGES[-1][0], RANGES[-1][1])
+        nc.vector.reciprocal(out=rstd[:], in_=std[:])
+        nc.vector.tensor_scalar(
+            out=cmat[:, 0:1], in0=mv[:, 0:1], scalar1=rstd[:, 0:1], scalar2=-1.0, op0=ALU.mult, op1=ALU.mult
+        )
+        nc.vector.tensor_scalar(
+            out=c32[:], in0=mv[:, 0:1], scalar1=rstd[:, 0:1], scalar2=-1.0, op0=ALU.mult, op1=ALU.mult
+        )
+        nc.vector.tensor_tensor(out=cmat[:, 1:2], in0=c32[:], in1=cmat[:, 0:1], op=ALU.subtract)
+        nc.vector.tensor_tensor(out=r1[:], in0=c32[:], in1=cmat[:, 0:1], op=ALU.subtract)
+        nc.vector.tensor_tensor(out=cmat[:, 2:3], in0=r1[:], in1=cmat[:, 1:2], op=ALU.subtract)
+        tp = psum.tile([P, P], BF16, name="tp", tag="bank")
+        nc.tensor.transpose(tp[:], cmat[:], ident_b[:])
+        nc.scalar.copy(out=lt[:], in_=tp[:])
+        for j in range(DO // 512):
+            cols = slice(512 * j, 512 * (j + 1))
+            shift = psum.tile([P, 512], F32, name="shift", tag="bank")
+            nc.tensor.matmul(out=shift[:], lhsT=lt[:], rhs=vmat[:, cols], start=True, stop=True)
+            nc.vector.scalar_tensor_tensor(
+                out=hg[:, cols], in0=hg[:, cols], scalar=rstd[:, 0:1], in1=shift[:], op0=ALU.mult, op1=ALU.add
+            )
+            nc.sync.dma_start(out=of[:, cols], in_=hg[:, cols])

@@ -19,7 +19,13 @@ G = DI // 512
 LN_EPS = 1e-5
 FLOPS = 2 * P * DI * DO
 
-RANGES = ((0, 2048, 1), (2048, 1024, 2), (3072, 512, 4), (3584, 256, 4), (3840, 256, 2))
+RANGES = (
+    (0, (512, 512, 512, 512), (1, 1, 1, 1, 1, 1, 1, 1)),
+    (2048, (512, 512, 128), (2, 2, 2, 2)),
+    (3200, (512, 128), (4, 4)),
+    (3840, (256,), (4, 2, 2)),
+)
+LATE = 2
 
 
 def tile_onebitlinear_w_kernel(
@@ -32,8 +38,8 @@ def tile_onebitlinear_w_kernel(
 
     with ExitStack() as ctx:
         const = ctx.enter_context(tc.tile_pool(name="const", bufs=1))
-        wpool = ctx.enter_context(tc.tile_pool(name="wpool", bufs=12))
-        work = ctx.enter_context(tc.tile_pool(name="work", bufs=3))
+        wpool = ctx.enter_context(tc.tile_pool(name="wpool", bufs=1))
+        work = ctx.enter_context(tc.tile_pool(name="work", bufs=4))
         psum = ctx.enter_context(tc.psum_pool(name="psum", bufs=8))
         ctx.enter_context(tc.manual_schedule())
 
@@ -56,7 +62,7 @@ def tile_onebitlinear_w_kernel(
         bias_bc = const.tile([P, DO], BF16)
         gamma_bc = const.tile([P, DO], BF16)
         hg = const.tile([P, DO], F32)
-        n_chunks = sum(max(1, w // 512) for (n0, w, gpd) in RANGES)
+        n_chunks = sum(len(widths) for (n0, widths, loads) in RANGES)
         stats = const.tile([P, n_chunks, 6], F32)
         mv = const.tile([P, 2], F32)
         std = const.tile([P, 1], F32)
@@ -175,41 +181,45 @@ def tile_onebitlinear_w_kernel(
             nc.vector.tensor_tensor(out=hg[:, cols], in0=h[:, 0:width], in1=gamma_bc[:, cols], op=ALU.mult)
 
         chunk = 0
-        last_h = None
-        for ri, (n0, w, gpd) in enumerate(RANGES):
-            nt = min(512, w)
+        late = []
+        for ri, (n0, widths, loads) in enumerate(RANGES):
+            w = sum(widths)
+            starts = [sum(widths[:j]) for j in range(len(widths))]
             accs = []
-            for j in range(w // nt):
+            for j, nt in enumerate(widths):
                 acc = psum.tile([P, nt], F32, name="acc", tag="bank")
                 accs.append(acc)
-            for g0 in range(0, G, gpd):
-                wt = wpool.tile([P, gpd, w], U32, name="wt", tag="wt", align_bytes=64)
+            g0 = 0
+            for li, gpd in enumerate(loads):
+                wt = wpool.tile([P, gpd, w], U32, name="wt%d_%d" % (ri, li), align_bytes=64)
                 nc.sync.dma_start(
                     out=wt[:].bitcast(I32), in_=w_view[:, g0 : g0 + gpd, 4 * n0 : 4 * (n0 + w)].bitcast(I32)
                 )
                 for gi in range(gpd):
                     g = g0 + gi
-                    for j in range(w // nt):
+                    for j, nt in enumerate(widths):
+                        c0 = starts[j]
                         nc.tensor.matmul_mx(
                             out=accs[j][:],
                             lhsT=xcodes[:, P * g : P * (g + 1)].bitcast(FP8X4),
                             lhsT_scale=xscales[:, P * g : P * (g + 1)],
-                            rhs=wt[:, gi, nt * j : nt * (j + 1)].bitcast(FP8X4),
-                            rhs_scale=planes[4 * (g % 4) : P, g // 4, n0 + nt * j : n0 + nt * (j + 1)],
+                            rhs=wt[:, gi, c0 : c0 + nt].bitcast(FP8X4),
+                            rhs_scale=planes[4 * (g % 4) : P, g // 4, n0 + c0 : n0 + c0 + nt],
                             start=(g == 0),
                             stop=(g == G - 1),
                         )
-            for j in range(w // nt):
-                h = to_h(accs[j][:], n0 + nt * j, nt, chunk)
+                g0 += gpd
+            for j, nt in enumerate(widths):
+                h = to_h(accs[j][:], n0 + starts[j], nt, chunk)
                 chunk += 1
-                if ri == len(RANGES) - 1:
-                    last_h = h
+                if ri >= len(RANGES) - LATE:
+                    late.append((h, n0 + starts[j], nt))
                 else:
-                    to_hg(h, n0 + nt * j, nt)
+                    to_hg(h, n0 + starts[j], nt)
 
         nc.vector.bn_aggr(out=mv[:], in_=stats[:].rearrange("p c s -> p (c s)"))
         nc.scalar.activation(out=std[:], in_=mv[:, 1:2], func=ACT.Sqrt, bias=eps[:, 0:1], scale=1.0)
-        to_hg(last_h, RANGES[-1][0], RANGES[-1][1])
+        to_hg(*late[-1])
         nc.vector.reciprocal(out=rstd[:], in_=std[:])
         nc.vector.tensor_scalar(
             out=cmat[:, 0:1], in0=mv[:, 0:1], scalar1=rstd[:, 0:1], scalar2=-1.0, op0=ALU.mult, op1=ALU.mult
@@ -220,6 +230,8 @@ def tile_onebitlinear_w_kernel(
         nc.vector.tensor_tensor(out=cmat[:, 1:2], in0=c32[:], in1=cmat[:, 0:1], op=ALU.subtract)
         nc.vector.tensor_tensor(out=r1[:], in0=c32[:], in1=cmat[:, 0:1], op=ALU.subtract)
         nc.vector.tensor_tensor(out=cmat[:, 2:3], in0=r1[:], in1=cmat[:, 1:2], op=ALU.subtract)
+        for item in late[:-1]:
+            to_hg(*item)
         tp = psum.tile([P, P], BF16, name="tp", tag="bank")
         nc.tensor.transpose(tp[:], cmat[:], ident_b[:])
         nc.scalar.copy(out=lt[:], in_=tp[:])

@@ -20,9 +20,11 @@ LN_EPS = 1e-5
 FLOPS = 2 * P * DI * DO
 
 RANGES = (
-    (0, (512, 512, 512, 512), (1, 1, 1, 1, 1, 1, 1, 1)),
-    (2048, (512, 512, 128), (2, 2, 2, 2)),
-    (3200, (512, 128), (4, 4)),
+    (0, (512, 512), (2, 2, 2, 2)),
+    (1024, (512, 512), (2, 2, 2, 2)),
+    (2048, (512, 512), (2, 2, 2, 2)),
+    (3072, (512,), (4, 4)),
+    (3584, (256,), (8,)),
     (3840, (256,), (4, 2, 2)),
 )
 LATE = 2
@@ -110,18 +112,15 @@ def tile_onebitlinear_w_kernel(
             out=ics_t[:].rearrange("p (g u) -> p g u", u=2), in_=pi[:, :, 0:G].rearrange("p u g -> p g u")
         )
 
-        def spread(v, dst):
-            dst_words = dst[:].bitcast(F32)
-            for c in range(4):
+        def spread(c):
+            for v, dst in enumerate((ocs_bc, bias_bc, gamma_bc)):
                 pb = psum.tile([P, 512], F32, name="pb", tag="bank")
                 for i in range(4):
                     col = 16 * v + 4 * c + i
                     nc.tensor.transpose(
                         pb[:, P * i : P * (i + 1)], vcol[:, col : col + 1].to_broadcast([P, P]), ident_f[:]
                     )
-                nc.scalar.copy(out=dst_words[:, 512 * c : 512 * (c + 1)], in_=pb[:])
-
-        spread(0, ocs_bc)
+                nc.scalar.copy(out=dst[:].bitcast(F32)[:, 512 * c : 512 * (c + 1)], in_=pb[:])
 
         x_words = x_sb[:].bitcast(F32)
         ics_bf = ics_t[:].bitcast(BF16)
@@ -164,8 +163,6 @@ def tile_onebitlinear_w_kernel(
         scale_x(7)
         quantise_x(1)
 
-        spread(1, bias_bc)
-        spread(2, gamma_bc)
 
         def to_h(acc, n0, width, chunk):
             cols = slice(n0, n0 + width)
@@ -183,6 +180,8 @@ def tile_onebitlinear_w_kernel(
         chunk = 0
         late = []
         for ri, (n0, widths, loads) in enumerate(RANGES):
+            if n0 % 1024 == 0:
+                spread(n0 // 1024)
             w = sum(widths)
             starts = [sum(widths[:j]) for j in range(len(widths))]
             accs = []

@@ -20,14 +20,13 @@ LN_EPS = 1e-5
 FLOPS = 2 * P * DI * DO
 
 RANGES = (
-    (0, (512, 512), (2, 2, 2, 2)),
-    (1024, (512, 512), (2, 2, 2, 2)),
-    (2048, (512, 512), (2, 2, 2, 2)),
-    (3072, (512,), (4, 4)),
-    (3584, (256,), (8,)),
-    (3840, (256,), (4, 2, 2)),
+    (0, (512, 512), (2, 2, 2, 2), ()),
+    (1024, (512, 512, 512), (2, 2, 2, 2), (1, 2)),
+    (2560, (512, 256, 128), (2, 2, 2, 2), (3,)),
+    (3456, (256, 128), (4, 4), ()),
+    (3840, (256,), (4, 2, 2), ()),
 )
-LATE = 2
+N_EARLY = 3840
 
 
 def tile_onebitlinear_w_kernel(
@@ -41,7 +40,6 @@ def tile_onebitlinear_w_kernel(
     with ExitStack() as ctx:
         const = ctx.enter_context(tc.tile_pool(name="const", bufs=1))
         wpool = ctx.enter_context(tc.tile_pool(name="wpool", bufs=1))
-        work = ctx.enter_context(tc.tile_pool(name="work", bufs=4))
         psum = ctx.enter_context(tc.psum_pool(name="psum", bufs=8))
         ctx.enter_context(tc.manual_schedule())
 
@@ -64,46 +62,39 @@ def tile_onebitlinear_w_kernel(
         bias_bc = const.tile([P, DO], BF16)
         gamma_bc = const.tile([P, DO], BF16)
         hg = const.tile([P, DO], F32)
-        n_chunks = sum(len(widths) for (n0, widths, loads) in RANGES)
-        stats = const.tile([P, n_chunks, 6], F32)
+        n_early = sum(len(r[1]) for r in RANGES[:-1])
+        stats = const.tile([P, n_early, 6], F32)
+        fin = const.tile([P, 15], F32)
+        mv0 = const.tile([P, 2], F32)
         mv = const.tile([P, 2], F32)
-        std = const.tile([P, 1], F32)
+        dm = const.tile([P, 1], F32)
         rstd = const.tile([P, 1], F32)
         c32 = const.tile([P, 1], F32)
-        r1 = const.tile([P, 1], F32)
         lt = const.tile([P, P], BF16)
 
-        nc.sync.dma_start(out=x_sb[:], in_=xf)
-
-        nc.vector.memset(eps[:], LN_EPS)
         nc.vector.memset(ics_rows[:].bitcast(I32), 0)
-        nc.vector.memset(vrow[:].bitcast(I32), 0)
         nc.vector.memset(planes[:].rearrange("p a n -> p (a n)").bitcast(I32), 0)
+        nc.vector.memset(eps[:], LN_EPS)
+        nc.vector.memset(vrow[:].bitcast(I32), 0)
         nc.vector.memset(vmat[:].bitcast(I32), 0)
         nc.vector.memset(cmat[:].bitcast(I32), 0)
-        nc.vector.memset(cmat[:, 3:4], 1.0)
+        nc.vector.memset(cmat[:, 2:3], 1.0)
+        nc.vector.memset(fin[:, 0:1], float(N_EARLY))
 
         make_identity(nc, ident_f[:])
         make_identity(nc, ident_b[:])
 
-        nc.scalar.dma_start(out=ics_rows[0:G, :], in_=in_channel_scale.rearrange("(g c) -> g c", g=G))
-        nc.scalar.dma_start(out=vrow[0:16, :], in_=out_channel_scale.rearrange("(j c) -> j c", j=16))
-        nc.scalar.dma_start(out=vrow[16:32, :], in_=bias.rearrange("(j c) -> j c", j=16))
-        nc.scalar.dma_start(out=vrow[32:48, :], in_=ln_gamma.rearrange("(j c) -> j c", j=16))
-        nc.scalar.activation(out=dummy[:], in_=eps[:], func=ACT.Sqrt)
-        nc.scalar.dma_start(out=vmat[0:3, :], in_=ln_gamma.partition_broadcast(3))
-        nc.scalar.dma_start(out=vmat[3:4, :], in_=ln_beta.rearrange("(o n) -> o n", o=1))
+        nc.scalar.activation(out=dummy[:], in_=eps[:], func=ACT.Abs_reciprocal_sqrt)
 
+        nc.sync.dma_start(out=ics_rows[0:G, :], in_=in_channel_scale.rearrange("(g c) -> g c", g=G))
+        nc.sync.dma_start(out=x_sb[:], in_=xf)
         for a in range(2):
-            for q in range(4):
+            for q in (0, 2, 1, 3):
                 nc.sync.dma_start(
                     out=planes[32 * q : 32 * q + 16, a, :].bitcast(I32),
                     in_=weight_scales[4 * a : 4 * a + 4, 4 * q : 4 * q + 4, :].bitcast(I32),
                 )
 
-        pv = psum.tile([P, P], F32, name="pv", tag="bank")
-        nc.tensor.transpose(pv[:], vrow[:].bitcast(F32), ident_f[:])
-        nc.scalar.copy(out=vcol[:], in_=pv[:])
         pi = psum.tile([P, 2, P], F32, name="pi", tag="bank")
         ics_words = ics_rows[:].bitcast(F32)
         for u in range(2):
@@ -111,6 +102,20 @@ def tile_onebitlinear_w_kernel(
         nc.scalar.copy(
             out=ics_t[:].rearrange("p (g u) -> p g u", u=2), in_=pi[:, :, 0:G].rearrange("p u g -> p g u")
         )
+
+        def load_vectors():
+            nc.sync.dma_start(out=vrow[0:16, :], in_=out_channel_scale.rearrange("(j c) -> j c", j=16))
+            nc.sync.dma_start(out=vrow[16:32, :], in_=bias.rearrange("(j c) -> j c", j=16))
+            nc.sync.dma_start(out=vrow[32:48, :], in_=ln_gamma.rearrange("(j c) -> j c", j=16))
+
+        def load_shift_rows():
+            nc.sync.dma_start(out=vmat[0:2, :], in_=ln_gamma.partition_broadcast(2))
+            nc.sync.dma_start(out=vmat[2:3, :], in_=ln_beta.rearrange("(o n) -> o n", o=1))
+
+        def vectors_to_columns():
+            pv = psum.tile([P, P], F32, name="pv", tag="bank")
+            nc.tensor.transpose(pv[:], vrow[:].bitcast(F32), ident_f[:])
+            nc.scalar.copy(out=vcol[:], in_=pv[:])
 
         def spread(c):
             for v, dst in enumerate((ocs_bc, bias_bc, gamma_bc)):
@@ -163,25 +168,29 @@ def tile_onebitlinear_w_kernel(
         scale_x(7)
         quantise_x(1)
 
-
-        def to_h(acc, n0, width, chunk):
+        def times_ocs(acc, n0, width):
             cols = slice(n0, n0 + width)
-            t1 = work.tile([P, 512], F32, name="t1", tag="t1")
-            h = work.tile([P, 512], F32, name="h", tag="h")
-            nc.vector.tensor_tensor(out=t1[:, 0:width], in0=acc, in1=ocs_bc[:, cols], op=ALU.mult)
-            nc.vector.tensor_tensor(out=h[:, 0:width], in0=t1[:, 0:width], in1=bias_bc[:, cols], op=ALU.add)
-            nc.vector.bn_stats(out=stats[:, chunk, :], in_=h[:, 0:width])
-            return h
+            nc.vector.tensor_tensor(out=hg[:, cols], in0=acc, in1=ocs_bc[:, cols], op=ALU.mult)
 
-        def to_hg(h, n0, width):
+        def plus_bias(n0, width):
             cols = slice(n0, n0 + width)
-            nc.vector.tensor_tensor(out=hg[:, cols], in0=h[:, 0:width], in1=gamma_bc[:, cols], op=ALU.mult)
+            nc.vector.tensor_tensor(out=hg[:, cols], in0=hg[:, cols], in1=bias_bc[:, cols], op=ALU.add)
 
-        chunk = 0
-        late = []
-        for ri, (n0, widths, loads) in enumerate(RANGES):
-            if n0 % 1024 == 0:
-                spread(n0 // 1024)
+        def centre_times_gamma(n0, width):
+            cols = slice(n0, n0 + width)
+            nc.vector.scalar_tensor_tensor(
+                out=hg[:, cols],
+                in0=hg[:, cols],
+                scalar=mv0[:, 0:1],
+                in1=gamma_bc[:, cols],
+                op0=ALU.subtract,
+                op1=ALU.mult,
+            )
+
+        def product(ri, after_load=None):
+            n0, widths, loads, blocks = RANGES[ri]
+            for c in blocks:
+                spread(c)
             w = sum(widths)
             starts = [sum(widths[:j]) for j in range(len(widths))]
             accs = []
@@ -208,29 +217,73 @@ def tile_onebitlinear_w_kernel(
                             stop=(g == G - 1),
                         )
                 g0 += gpd
-            for j, nt in enumerate(widths):
-                h = to_h(accs[j][:], n0 + starts[j], nt, chunk)
-                chunk += 1
-                if ri >= len(RANGES) - LATE:
-                    late.append((h, n0 + starts[j], nt))
-                else:
-                    to_hg(h, n0 + starts[j], nt)
+                if after_load is not None:
+                    after_load(li)
+            return [(accs[j], n0 + starts[j], nt) for j, nt in enumerate(widths)]
 
-        nc.vector.bn_aggr(out=mv[:], in_=stats[:].rearrange("p c s -> p (c s)"))
-        nc.scalar.activation(out=std[:], in_=mv[:, 1:2], func=ACT.Sqrt, bias=eps[:, 0:1], scale=1.0)
-        to_hg(*late[-1])
-        nc.vector.reciprocal(out=rstd[:], in_=std[:])
+        def to_stats(parts, first_slot):
+            for acc, n0, nt in parts:
+                times_ocs(acc[:], n0, nt)
+            for acc, n0, nt in parts:
+                plus_bias(n0, nt)
+            for i, (acc, n0, nt) in enumerate(parts):
+                nc.vector.bn_stats(out=stats[:, first_slot + i, :], in_=hg[:, n0 : n0 + nt])
+
+        def in_first_range(li):
+            if li == 0:
+                load_vectors()
+                vectors_to_columns()
+                spread(0)
+            if li == 3:
+                load_shift_rows()
+
+        parts = product(0, in_first_range)
+        to_stats(parts, 0)
+        nc.vector.bn_aggr(out=mv0[:], in_=stats[:, 0, :])
+        for acc, n0, nt in parts:
+            centre_times_gamma(n0, nt)
+
+        parts = product(1)
+        to_stats(parts, 2)
+        for acc, n0, nt in parts:
+            centre_times_gamma(n0, nt)
+
+        parts = product(2)
+        to_stats(parts, 5)
+        for acc, n0, nt in parts:
+            centre_times_gamma(n0, nt)
+
+        parts = product(3)
+        to_stats(parts, 8)
+        nc.vector.bn_aggr(out=fin[:, 1:3], in_=stats[:].rearrange("p c s -> p (c s)"))
         nc.vector.tensor_scalar(
-            out=cmat[:, 0:1], in0=mv[:, 0:1], scalar1=rstd[:, 0:1], scalar2=-1.0, op0=ALU.mult, op1=ALU.mult
+            out=fin[:, 2:3], in0=fin[:, 2:3], scalar1=float(N_EARLY), scalar2=None, op0=ALU.mult
         )
+
+        fill = [(3456 + P * i, P) for i in range(5)]
+
+        last = product(4)[0][0]
+        for i in range(2):
+            times_ocs(last[:, P * i : P * (i + 1)], 3840 + P * i, P)
+        for i in range(2):
+            plus_bias(3840 + P * i, P)
+        for i in range(2):
+            nc.vector.bn_stats(out=fin[:, 3 + 6 * i : 9 + 6 * i], in_=hg[:, 3840 + P * i : 3840 + P * (i + 1)])
+
+        centre_times_gamma(*fill[0])
+        nc.vector.bn_aggr(out=mv[:], in_=fin[:])
+        nc.scalar.activation(out=rstd[:], in_=mv[:, 1:2], func=ACT.Abs_reciprocal_sqrt, bias=eps[:, 0:1], scale=1.0)
+        centre_times_gamma(*fill[1])
         nc.vector.tensor_scalar(
-            out=c32[:], in0=mv[:, 0:1], scalar1=rstd[:, 0:1], scalar2=-1.0, op0=ALU.mult, op1=ALU.mult
+            out=dm[:], in0=mv[:, 0:1], scalar1=mv0[:, 0:1], scalar2=-1.0, op0=ALU.subtract, op1=ALU.mult
         )
+        centre_times_gamma(*fill[2])
+        nc.vector.tensor_scalar(out=cmat[:, 0:1], in0=dm[:], scalar1=rstd[:, 0:1], scalar2=None, op0=ALU.mult)
+        nc.vector.tensor_scalar(out=c32[:], in0=dm[:], scalar1=rstd[:, 0:1], scalar2=None, op0=ALU.mult)
+        centre_times_gamma(*fill[3])
         nc.vector.tensor_tensor(out=cmat[:, 1:2], in0=c32[:], in1=cmat[:, 0:1], op=ALU.subtract)
-        nc.vector.tensor_tensor(out=r1[:], in0=c32[:], in1=cmat[:, 0:1], op=ALU.subtract)
-        nc.vector.tensor_tensor(out=cmat[:, 2:3], in0=r1[:], in1=cmat[:, 1:2], op=ALU.subtract)
-        for item in late[:-1]:
-            to_hg(*item)
+        for item in fill[4:]:
+            centre_times_gamma(*item)
         tp = psum.tile([P, P], BF16, name="tp", tag="bank")
         nc.tensor.transpose(tp[:], cmat[:], ident_b[:])
         nc.scalar.copy(out=lt[:], in_=tp[:])

@@ -86,8 +86,8 @@ def tile_onebitlinear_w_kernel(
 
         nc.scalar.activation(out=dummy[:], in_=eps[:], func=ACT.Abs_reciprocal_sqrt)
 
-        nc.sync.dma_start(out=ics_rows[0:G, :], in_=in_channel_scale.rearrange("(g c) -> g c", g=G))
         nc.sync.dma_start(out=x_sb[:], in_=xf)
+        nc.sync.dma_start(out=ics_rows[0:G, :], in_=in_channel_scale.rearrange("(g c) -> g c", g=G))
         for a in range(2):
             for q in (0, 2, 1, 3):
                 nc.sync.dma_start(
@@ -287,9 +287,10 @@ def tile_onebitlinear_w_kernel(
         tp = psum.tile([P, P], BF16, name="tp", tag="bank")
         nc.tensor.transpose(tp[:], cmat[:], ident_b[:])
         nc.scalar.copy(out=lt[:], in_=tp[:])
-        for j in range(DO // 512):
-            cols = slice(512 * j, 512 * (j + 1))
-            shift = psum.tile([P, 512], F32, name="shift", tag="bank")
+        widths = (256, 256) + (512,) * (DO // 512 - 2) + (256, 256)
+        for j, width in enumerate(widths):
+            cols = slice(sum(widths[:j]), sum(widths[:j]) + width)
+            shift = psum.tile([P, width], F32, name="shift", tag="bank")
             nc.tensor.matmul(out=shift[:], lhsT=lt[:], rhs=vmat[:, cols], start=True, stop=True)
             nc.vector.scalar_tensor_tensor(
                 out=hg[:, cols], in0=hg[:, cols], scalar=rstd[:, 0:1], in1=shift[:], op0=ALU.mult, op1=ALU.add

@@ -71,6 +71,8 @@ def tile_onebitlinear_w_kernel(
         rstd = const.tile([P, 1], F32)
         c32 = const.tile([P, 1], F32)
         lt = const.tile([P, P], BF16)
+        beta_first = const.tile([P, 256], BF16)
+        y_first = const.tile([P, 256], F32)
 
         nc.vector.memset(ics_rows[:].bitcast(I32), 0)
         nc.vector.memset(planes[:].rearrange("p a n -> p (a n)").bitcast(I32), 0)
@@ -107,6 +109,7 @@ def tile_onebitlinear_w_kernel(
             nc.sync.dma_start(out=vrow[0:16, :], in_=out_channel_scale.rearrange("(j c) -> j c", j=16))
             nc.sync.dma_start(out=vrow[16:32, :], in_=bias.rearrange("(j c) -> j c", j=16))
             nc.sync.dma_start(out=vrow[32:48, :], in_=ln_gamma.rearrange("(j c) -> j c", j=16))
+            nc.sync.dma_start(out=vrow[48:49, :], in_=ln_beta[0:256].rearrange("(o c) -> o c", o=1))
 
         def load_shift_rows():
             nc.sync.dma_start(out=vmat[0:2, :], in_=ln_gamma.partition_broadcast(2))
@@ -234,6 +237,9 @@ def tile_onebitlinear_w_kernel(
                 load_vectors()
                 vectors_to_columns()
                 spread(0)
+                pf = psum.tile([P, P], F32, name="pf", tag="bank")
+                nc.tensor.transpose(pf[:], vcol[:, 48:49].to_broadcast([P, P]), ident_f[:])
+                nc.scalar.copy(out=beta_first[:].bitcast(F32), in_=pf[:])
             if li == 3:
                 load_shift_rows()
 
@@ -282,14 +288,21 @@ def tile_onebitlinear_w_kernel(
         nc.vector.tensor_scalar(out=c32[:], in0=dm[:], scalar1=rstd[:, 0:1], scalar2=None, op0=ALU.mult)
         centre_times_gamma(*fill[3])
         nc.vector.tensor_tensor(out=cmat[:, 1:2], in0=c32[:], in1=cmat[:, 0:1], op=ALU.subtract)
-        for item in fill[4:]:
-            centre_times_gamma(*item)
         tp = psum.tile([P, P], BF16, name="tp", tag="bank")
         nc.tensor.transpose(tp[:], cmat[:], ident_b[:])
         nc.scalar.copy(out=lt[:], in_=tp[:])
-        widths = (256, 256) + (512,) * (DO // 512 - 2) + (256, 256)
+        nc.vector.scalar_tensor_tensor(
+            out=y_first[:], in0=gamma_bc[:, 0:256], scalar=c32[:, 0:1], in1=beta_first[:], op0=ALU.mult, op1=ALU.add
+        )
+        centre_times_gamma(*fill[4])
+        nc.vector.scalar_tensor_tensor(
+            out=hg[:, 0:256], in0=hg[:, 0:256], scalar=rstd[:, 0:1], in1=y_first[:], op0=ALU.mult, op1=ALU.add
+        )
+        nc.sync.dma_start(out=of[:, 0:256], in_=hg[:, 0:256])
+        widths = (256,) + (512,) * (DO // 512 - 2) + (256, 256)
         for j, width in enumerate(widths):
-            cols = slice(sum(widths[:j]), sum(widths[:j]) + width)
+            c0 = 256 + sum(widths[:j])
+            cols = slice(c0, c0 + width)
             shift = psum.tile([P, width], F32, name="shift", tag="bank")
             nc.tensor.matmul(out=shift[:], lhsT=lt[:], rhs=vmat[:, cols], start=True, stop=True)
             nc.vector.scalar_tensor_tensor(

@@ -20,13 +20,13 @@ LN_EPS = 1e-5
 FLOPS = 2 * P * DI * DO
 
 RANGES = (
-    (0, (512, 512), (2, 2, 2, 2), ()),
-    (1024, (512, 512, 512), (2, 2, 2, 2), (1, 2)),
-    (2560, (512, 256, 128), (2, 2, 2, 2), (3,)),
-    (3456, (256, 128), (4, 4), ()),
+    (0, (512, 512, 512, 256), (2, 2, 2, 2), ()),
+    (1792, (512, 512), (2, 2, 2, 2), (2,)),
+    (2816, (512, 128), (2, 2, 2, 2), (3,)),
+    (3456, (256, 128), (4, 2, 2), ()),
     (3840, (256,), (4, 2, 2), ()),
 )
-N_EARLY = 3840
+N_EARLY = 2816
 
 
 def tile_onebitlinear_w_kernel(
@@ -40,7 +40,8 @@ def tile_onebitlinear_w_kernel(
     with ExitStack() as ctx:
         const = ctx.enter_context(tc.tile_pool(name="const", bufs=1))
         wpool = ctx.enter_context(tc.tile_pool(name="wpool", bufs=1))
-        psum = ctx.enter_context(tc.psum_pool(name="psum", bufs=8))
+        pacc = ctx.enter_context(tc.psum_pool(name="pacc", bufs=5))
+        paux = ctx.enter_context(tc.psum_pool(name="paux", bufs=3))
         ctx.enter_context(tc.manual_schedule())
 
         eps = const.tile([P, 1], F32)
@@ -62,9 +63,9 @@ def tile_onebitlinear_w_kernel(
         bias_bc = const.tile([P, DO], BF16)
         gamma_bc = const.tile([P, DO], BF16)
         hg = const.tile([P, DO], F32)
-        n_early = sum(len(r[1]) for r in RANGES[:-1])
+        n_early = sum(len(r[1]) for r in RANGES[:2])
         stats = const.tile([P, n_early, 6], F32)
-        fin = const.tile([P, 15], F32)
+        fin = const.tile([P, 39], F32)
         mv0 = const.tile([P, 2], F32)
         mv = const.tile([P, 2], F32)
         dm = const.tile([P, 1], F32)
@@ -84,6 +85,12 @@ def tile_onebitlinear_w_kernel(
         nc.vector.memset(fin[:, 0:1], float(N_EARLY))
 
         make_identity(nc, ident_f[:])
+        for a in range(2):
+            for q in (2, 3):
+                nc.gpsimd.dma_start(
+                    out=planes[32 * q : 32 * q + 16, a, :].bitcast(F32),
+                    in_=weight_scales[4 * a : 4 * a + 4, 4 * q : 4 * q + 4, :].bitcast(F32),
+                )
         make_identity(nc, ident_b[:])
 
         nc.scalar.activation(out=dummy[:], in_=eps[:], func=ACT.Abs_reciprocal_sqrt)
@@ -91,13 +98,13 @@ def tile_onebitlinear_w_kernel(
         nc.sync.dma_start(out=x_sb[:], in_=xf)
         nc.sync.dma_start(out=ics_rows[0:G, :], in_=in_channel_scale.rearrange("(g c) -> g c", g=G))
         for a in range(2):
-            for q in (0, 2, 1, 3):
+            for q in (0, 1):
                 nc.sync.dma_start(
                     out=planes[32 * q : 32 * q + 16, a, :].bitcast(I32),
                     in_=weight_scales[4 * a : 4 * a + 4, 4 * q : 4 * q + 4, :].bitcast(I32),
                 )
 
-        pi = psum.tile([P, 2, P], F32, name="pi", tag="bank")
+        pi = paux.tile([P, 2, P], F32, name="pi", tag="aux")
         ics_words = ics_rows[:].bitcast(F32)
         for u in range(2):
             nc.tensor.transpose(pi[:, u, :], ics_words[:, u : 256 : 2], ident_f[:])
@@ -116,13 +123,13 @@ def tile_onebitlinear_w_kernel(
             nc.sync.dma_start(out=vmat[2:3, :], in_=ln_beta.rearrange("(o n) -> o n", o=1))
 
         def vectors_to_columns():
-            pv = psum.tile([P, P], F32, name="pv", tag="bank")
+            pv = paux.tile([P, P], F32, name="pv", tag="aux")
             nc.tensor.transpose(pv[:], vrow[:].bitcast(F32), ident_f[:])
             nc.scalar.copy(out=vcol[:], in_=pv[:])
 
         def spread(c):
             for v, dst in enumerate((ocs_bc, bias_bc, gamma_bc)):
-                pb = psum.tile([P, 512], F32, name="pb", tag="bank")
+                pb = paux.tile([P, 512], F32, name="pb", tag="aux")
                 for i in range(4):
                     col = 16 * v + 4 * c + i
                     nc.tensor.transpose(
@@ -134,7 +141,7 @@ def tile_onebitlinear_w_kernel(
         ics_bf = ics_t[:].bitcast(BF16)
         xts = []
         for b in range(G // 2):
-            xt = psum.tile([P, 512], F32, name="xt", tag="bank")
+            xt = pacc.tile([P, 512], F32, name="xt", tag="acc")
             xts.append(xt)
             for h in range(2):
                 g = 2 * b + h
@@ -198,7 +205,7 @@ def tile_onebitlinear_w_kernel(
             starts = [sum(widths[:j]) for j in range(len(widths))]
             accs = []
             for j, nt in enumerate(widths):
-                acc = psum.tile([P, nt], F32, name="acc", tag="bank")
+                acc = pacc.tile([P, nt], F32, name="acc", tag="acc")
                 accs.append(acc)
             g0 = 0
             for li, gpd in enumerate(loads):
@@ -224,22 +231,27 @@ def tile_onebitlinear_w_kernel(
                     after_load(li)
             return [(accs[j], n0 + starts[j], nt) for j, nt in enumerate(widths)]
 
-        def to_stats(parts, first_slot):
+        def to_stats(parts, first_slot, late=False):
             for acc, n0, nt in parts:
                 times_ocs(acc[:], n0, nt)
             for acc, n0, nt in parts:
                 plus_bias(n0, nt)
             for i, (acc, n0, nt) in enumerate(parts):
-                nc.vector.bn_stats(out=stats[:, first_slot + i, :], in_=hg[:, n0 : n0 + nt])
+                k = first_slot + i
+                nc.vector.bn_stats(
+                    out=fin[:, 3 + 6 * k : 9 + 6 * k] if late else stats[:, k, :], in_=hg[:, n0 : n0 + nt]
+                )
 
         def in_first_range(li):
             if li == 0:
                 load_vectors()
                 vectors_to_columns()
                 spread(0)
-                pf = psum.tile([P, P], F32, name="pf", tag="bank")
+                pf = paux.tile([P, P], F32, name="pf", tag="aux")
                 nc.tensor.transpose(pf[:], vcol[:, 48:49].to_broadcast([P, P]), ident_f[:])
                 nc.scalar.copy(out=beta_first[:].bitcast(F32), in_=pf[:])
+            if li == 1:
+                spread(1)
             if li == 3:
                 load_shift_rows()
 
@@ -250,31 +262,34 @@ def tile_onebitlinear_w_kernel(
             centre_times_gamma(n0, nt)
 
         parts = product(1)
-        to_stats(parts, 2)
+        to_stats(parts, 4)
         for acc, n0, nt in parts:
             centre_times_gamma(n0, nt)
-
-        parts = product(2)
-        to_stats(parts, 5)
-        for acc, n0, nt in parts:
-            centre_times_gamma(n0, nt)
-
-        parts = product(3)
-        to_stats(parts, 8)
         nc.vector.bn_aggr(out=fin[:, 1:3], in_=stats[:].rearrange("p c s -> p (c s)"))
         nc.vector.tensor_scalar(
             out=fin[:, 2:3], in0=fin[:, 2:3], scalar1=float(N_EARLY), scalar2=None, op0=ALU.mult
         )
 
+        parts = product(2)
+        to_stats(parts, 0, late=True)
+        for acc, n0, nt in parts:
+            centre_times_gamma(n0, nt)
+
+        parts = product(3)
+        to_stats(parts, 2, late=True)
+
         fill = [(3456 + P * i, P) for i in range(5)]
 
         last = product(4)[0][0]
+        warm = paux.tile([P, 512], F32, name="warm", tag="aux")
+        for i in range(8):
+            nc.tensor.matmul(out=warm[:], lhsT=ident_b[:], rhs=gamma_bc[:, 0:512], start=True, stop=True)
         for i in range(2):
             times_ocs(last[:, P * i : P * (i + 1)], 3840 + P * i, P)
         for i in range(2):
             plus_bias(3840 + P * i, P)
         for i in range(2):
-            nc.vector.bn_stats(out=fin[:, 3 + 6 * i : 9 + 6 * i], in_=hg[:, 3840 + P * i : 3840 + P * (i + 1)])
+            nc.vector.bn_stats(out=fin[:, 27 + 6 * i : 33 + 6 * i], in_=hg[:, 3840 + P * i : 3840 + P * (i + 1)])
 
         centre_times_gamma(*fill[0])
         nc.vector.bn_aggr(out=mv[:], in_=fin[:])
@@ -288,7 +303,7 @@ def tile_onebitlinear_w_kernel(
         nc.vector.tensor_scalar(out=c32[:], in0=dm[:], scalar1=rstd[:, 0:1], scalar2=None, op0=ALU.mult)
         centre_times_gamma(*fill[3])
         nc.vector.tensor_tensor(out=cmat[:, 1:2], in0=c32[:], in1=cmat[:, 0:1], op=ALU.subtract)
-        tp = psum.tile([P, P], BF16, name="tp", tag="bank")
+        tp = paux.tile([P, P], BF16, name="tp", tag="aux")
         nc.tensor.transpose(tp[:], cmat[:], ident_b[:])
         nc.scalar.copy(out=lt[:], in_=tp[:])
         nc.vector.scalar_tensor_tensor(
@@ -303,7 +318,10 @@ def tile_onebitlinear_w_kernel(
         for j, width in enumerate(widths):
             c0 = 256 + sum(widths[:j])
             cols = slice(c0, c0 + width)
-            shift = psum.tile([P, width], F32, name="shift", tag="bank")
+            if j % 3 == 2:
+                shift = paux.tile([P, width], F32, name="shift", tag="aux")
+            else:
+                shift = pacc.tile([P, width], F32, name="shift", tag="acc")
             nc.tensor.matmul(out=shift[:], lhsT=lt[:], rhs=vmat[:, cols], start=True, stop=True)
             nc.vector.scalar_tensor_tensor(
                 out=hg[:, cols], in0=hg[:, cols], scalar=rstd[:, 0:1], in1=shift[:], op0=ALU.mult, op1=ALU.add

from contextlib import ExitStack

import concourse.mybir as mybir
from concourse.masks import make_identity

F32 = mybir.dt.float32
BF16 = mybir.dt.bfloat16
I32 = mybir.dt.int32
U32 = mybir.dt.uint32
U8 = mybir.dt.uint8
FP8X4 = mybir.dt.float8_e4m3fn_x4
ALU = mybir.AluOpType
ACT = mybir.ActivationFunctionType

P = 128
DI = 4096
DO = 4096
G = DI // 512
LN_EPS = 1e-5
FLOPS = 2 * P * DI * DO

RANGES = (
    (0, (512, 512, 512, 256), (2, 2, 2, 2), ()),
    (1792, (512, 512), (2, 2, 2, 2), (2,)),
    (2816, (512, 128), (2, 2, 2, 2), (3,)),
    (3456, (256, 128), (4, 2, 2), ()),
    (3840, (256,), (4, 2, 2), ()),
)
N_EARLY = 2816


def tile_onebitlinear_w_kernel(
    tc, x, weight_words, weight_scales, in_channel_scale, out_channel_scale, bias, ln_gamma, ln_beta, out
):
    nc = tc.nc
    xf = x.flatten_outer_dims()
    of = out.flatten_outer_dims()
    w_view = weight_words.rearrange("g p n t -> p g (n t)")

    with ExitStack() as ctx:
        const = ctx.enter_context(tc.tile_pool(name="const", bufs=1))
        wpool = ctx.enter_context(tc.tile_pool(name="wpool", bufs=1))
        pacc = ctx.enter_context(tc.psum_pool(name="pacc", bufs=5))
        paux = ctx.enter_context(tc.psum_pool(name="paux", bufs=3))
        ctx.enter_context(tc.manual_schedule())

        eps = const.tile([P, 1], F32)
        dummy = const.tile([P, 1], F32)
        ics_rows = const.tile([P, 512], BF16)
        vrow = const.tile([P, 256], BF16)
        planes = const.tile([P, 2, DO], U8, align_bytes=64)
        vmat = const.tile([P, DO], BF16)
        cmat = const.tile([P, P], BF16)
        ident_f = const.tile([P, P], F32)
        ident_b = const.tile([P, P], BF16)
        x_sb = const.tile([P, DI], BF16)
        grouped = const.tile([P, DI], BF16, align_bytes=64)
        xcodes = const.tile([P, DI // 4], U32, align_bytes=64)
        xscales = const.tile([P, DI // 4], U8, align_bytes=64)
        vcol = const.tile([P, P], F32)
        ics_t = const.tile([P, 2 * G], F32)
        ocs_bc = const.tile([P, DO], BF16)
        bias_bc = const.tile([P, DO], BF16)
        gamma_bc = const.tile([P, DO], BF16)
        hg = const.tile([P, DO], F32)
        n_early = sum(len(r[1]) for r in RANGES[:2])
        stats = const.tile([P, n_early, 6], F32)
        fin = const.tile([P, 39], F32)
        mv0 = const.tile([P, 2], F32)
        mv = const.tile([P, 2], F32)
        dm = const.tile([P, 1], F32)
        rstd = const.tile([P, 1], F32)
        c32 = const.tile([P, 1], F32)
        lt = const.tile([P, P], BF16)
        beta_first = const.tile([P, 256], BF16)
        y_first = const.tile([P, 256], F32)

        nc.vector.memset(ics_rows[:].bitcast(I32), 0)
        nc.vector.memset(planes[:].rearrange("p a n -> p (a n)").bitcast(I32), 0)
        nc.vector.memset(eps[:], LN_EPS)
        nc.vector.memset(vrow[:].bitcast(I32), 0)
        nc.vector.memset(vmat[:].bitcast(I32), 0)
        nc.vector.memset(cmat[:].bitcast(I32), 0)
        nc.vector.memset(cmat[:, 2:3], 1.0)
        nc.vector.memset(fin[:, 0:1], float(N_EARLY))

        make_identity(nc, ident_f[:])
        for a in range(2):
            for q in (2, 3):
                nc.gpsimd.dma_start(
                    out=planes[32 * q : 32 * q + 16, a, :].bitcast(F32),
                    in_=weight_scales[4 * a : 4 * a + 4, 4 * q : 4 * q + 4, :].bitcast(F32),
                )
        make_identity(nc, ident_b[:])

        nc.scalar.activation(out=dummy[:], in_=eps[:], func=ACT.Abs_reciprocal_sqrt)

        nc.sync.dma_start(out=x_sb[:], in_=xf)
        nc.sync.dma_start(out=ics_rows[0:G, :], in_=in_channel_scale.rearrange("(g c) -> g c", g=G))
        for a in range(2):
            for q in (0, 1):
                nc.sync.dma_start(
                    out=planes[32 * q : 32 * q + 16, a, :].bitcast(I32),
                    in_=weight_scales[4 * a : 4 * a + 4, 4 * q : 4 * q + 4, :].bitcast(I32),
                )

        pi = paux.tile([P, 2, P], F32, name="pi", tag="aux")
        ics_words = ics_rows[:].bitcast(F32)
        for u in range(2):
            nc.tensor.transpose(pi[:, u, :], ics_words[:, u : 256 : 2], ident_f[:])
        nc.scalar.copy(
            out=ics_t[:].rearrange("p (g u) -> p g u", u=2), in_=pi[:, :, 0:G].rearrange("p u g -> p g u")
        )

        def load_vectors():
            nc.sync.dma_start(out=vrow[0:16, :], in_=out_channel_scale.rearrange("(j c) -> j c", j=16))
            nc.sync.dma_start(out=vrow[16:32, :], in_=bias.rearrange("(j c) -> j c", j=16))
            nc.sync.dma_start(out=vrow[32:48, :], in_=ln_gamma.rearrange("(j c) -> j c", j=16))
            nc.sync.dma_start(out=vrow[48:49, :], in_=ln_beta[0:256].rearrange("(o c) -> o c", o=1))

        def load_shift_rows():
            nc.sync.dma_start(out=vmat[0:2, :], in_=ln_gamma.partition_broadcast(2))
            nc.sync.dma_start(out=vmat[2:3, :], in_=ln_beta.rearrange("(o n) -> o n", o=1))

        def vectors_to_columns():
            pv = paux.tile([P, P], F32, name="pv", tag="aux")
            nc.tensor.transpose(pv[:], vrow[:].bitcast(F32), ident_f[:])
            nc.scalar.copy(out=vcol[:], in_=pv[:])

        def spread(c):
            for v, dst in enumerate((ocs_bc, bias_bc, gamma_bc)):
                pb = paux.tile([P, 512], F32, name="pb", tag="aux")
                for i in range(4):
                    col = 16 * v + 4 * c + i
                    nc.tensor.transpose(
                        pb[:, P * i : P * (i + 1)], vcol[:, col : col + 1].to_broadcast([P, P]), ident_f[:]
                    )
                nc.scalar.copy(out=dst[:].bitcast(F32)[:, 512 * c : 512 * (c + 1)], in_=pb[:])

        x_words = x_sb[:].bitcast(F32)
        ics_bf = ics_t[:].bitcast(BF16)
        xts = []
        for b in range(G // 2):
            xt = pacc.tile([P, 512], F32, name="xt", tag="acc")
            xts.append(xt)
            for h in range(2):
                g = 2 * b + h
                for u in range(2):
                    nc.tensor.transpose(
                        xt[:, 256 * h + P * u : 256 * h + P * (u + 1)],
                        x_words[:, 256 * g + u : 256 * (g + 1) : 2],
                        ident_f[:],
                    )

        def scale_x(g):
            src = xts[g // 2][:].bitcast(BF16)[:, 512 * (g % 2) : 512 * (g % 2 + 1)]
            nc.vector.tensor_tensor(
                out=grouped[:, 512 * g : 512 * (g + 1)].rearrange("p (r u e) -> p r u e", u=2, e=2),
                in0=src.rearrange("p (u r e) -> p r u e", u=2, e=2),
                in1=ics_bf[:, 4 * g : 4 * g + 4]
                .rearrange("p (u e) -> p u e", u=2)
                .unsqueeze(1)
                .to_broadcast([P, P, 2, 2]),
                op=ALU.mult,
            )

        def quantise_x(half):
            nc.vector.quantize_mx(
                out=xcodes[:, 512 * half : 512 * (half + 1)].bitcast(FP8X4),
                scales=xscales[:, 512 * half : 512 * (half + 1)],
                in_=grouped[:, 2048 * half : 2048 * (half + 1)],
            )

        for g in range(6):
            scale_x(g)
        quantise_x(0)
        scale_x(6)
        scale_x(7)
        quantise_x(1)

        def times_ocs(acc, n0, width):
            cols = slice(n0, n0 + width)
            nc.vector.tensor_tensor(out=hg[:, cols], in0=acc, in1=ocs_bc[:, cols], op=ALU.mult)

        def plus_bias(n0, width):
            cols = slice(n0, n0 + width)
            nc.vector.tensor_tensor(out=hg[:, cols], in0=hg[:, cols], in1=bias_bc[:, cols], op=ALU.add)

        def centre_times_gamma(n0, width):
            cols = slice(n0, n0 + width)
            nc.vector.scalar_tensor_tensor(
                out=hg[:, cols],
                in0=hg[:, cols],
                scalar=mv0[:, 0:1],
                in1=gamma_bc[:, cols],
                op0=ALU.subtract,
                op1=ALU.mult,
            )

        def product(ri, after_load=None):
            n0, widths, loads, blocks = RANGES[ri]
            for c in blocks:
                spread(c)
            w = sum(widths)
            starts = [sum(widths[:j]) for j in range(len(widths))]
            accs = []
            for j, nt in enumerate(widths):
                acc = pacc.tile([P, nt], F32, name="acc", tag="acc")
                accs.append(acc)
            g0 = 0
            for li, gpd in enumerate(loads):
                wt = wpool.tile([P, gpd, w], U32, name="wt%d_%d" % (ri, li), align_bytes=64)
                nc.sync.dma_start(
                    out=wt[:].bitcast(I32), in_=w_view[:, g0 : g0 + gpd, 4 * n0 : 4 * (n0 + w)].bitcast(I32)
                )
                for gi in range(gpd):
                    g = g0 + gi
                    for j, nt in enumerate(widths):
                        c0 = starts[j]
                        nc.tensor.matmul_mx(
                            out=accs[j][:],
                            lhsT=xcodes[:, P * g : P * (g + 1)].bitcast(FP8X4),
                            lhsT_scale=xscales[:, P * g : P * (g + 1)],
                            rhs=wt[:, gi, c0 : c0 + nt].bitcast(FP8X4),
                            rhs_scale=planes[4 * (g % 4) : P, g // 4, n0 + c0 : n0 + c0 + nt],
                            start=(g == 0),
                            stop=(g == G - 1),
                        )
                g0 += gpd
                if after_load is not None:
                    after_load(li)
            return [(accs[j], n0 + starts[j], nt) for j, nt in enumerate(widths)]

        def to_stats(parts, first_slot, late=False):
            for acc, n0, nt in parts:
                times_ocs(acc[:], n0, nt)
            for acc, n0, nt in parts:
                plus_bias(n0, nt)
            for i, (acc, n0, nt) in enumerate(parts):
                k = first_slot + i
                nc.vector.bn_stats(
                    out=fin[:, 3 + 6 * k : 9 + 6 * k] if late else stats[:, k, :], in_=hg[:, n0 : n0 + nt]
                )

        def in_first_range(li):
            if li == 0:
                load_vectors()
                vectors_to_columns()
                spread(0)
                pf = paux.tile([P, P], F32, name="pf", tag="aux")
                nc.tensor.transpose(pf[:], vcol[:, 48:49].to_broadcast([P, P]), ident_f[:])
                nc.scalar.copy(out=beta_first[:].bitcast(F32), in_=pf[:])
            if li == 1:
                spread(1)
            if li == 3:
                load_shift_rows()

        parts = product(0, in_first_range)
        to_stats(parts, 0)
        nc.vector.bn_aggr(out=mv0[:], in_=stats[:, 0, :])
        for acc, n0, nt in parts:
            centre_times_gamma(n0, nt)

        parts = product(1)
        to_stats(parts, 4)
        for acc, n0, nt in parts:
            centre_times_gamma(n0, nt)
        nc.vector.bn_aggr(out=fin[:, 1:3], in_=stats[:].rearrange("p c s -> p (c s)"))
        nc.vector.tensor_scalar(
            out=fin[:, 2:3], in0=fin[:, 2:3], scalar1=float(N_EARLY), scalar2=None, op0=ALU.mult
        )

        parts = product(2)
        to_stats(parts, 0, late=True)
        for acc, n0, nt in parts:
            centre_times_gamma(n0, nt)

        parts = product(3)
        to_stats(parts, 2, late=True)

        fill = [(3456 + P * i, P) for i in range(5)]

        last = product(4)[0][0]
        warm = paux.tile([P, 512], F32, name="warm", tag="aux")
        for i in range(8):
            nc.tensor.matmul(out=warm[:], lhsT=ident_b[:], rhs=gamma_bc[:, 0:512], start=True, stop=True)
        for i in range(2):
            times_ocs(last[:, P * i : P * (i + 1)], 3840 + P * i, P)
        for i in range(2):
            plus_bias(3840 + P * i, P)
        for i in range(2):
            nc.vector.bn_stats(out=fin[:, 27 + 6 * i : 33 + 6 * i], in_=hg[:, 3840 + P * i : 3840 + P * (i + 1)])

        centre_times_gamma(*fill[0])
        nc.vector.bn_aggr(out=mv[:], in_=fin[:])
        nc.scalar.activation(out=rstd[:], in_=mv[:, 1:2], func=ACT.Abs_reciprocal_sqrt, bias=eps[:, 0:1], scale=1.0)
        centre_times_gamma(*fill[1])
        nc.vector.tensor_scalar(
            out=dm[:], in0=mv[:, 0:1], scalar1=mv0[:, 0:1], scalar2=-1.0, op0=ALU.subtract, op1=ALU.mult
        )
        centre_times_gamma(*fill[2])
        nc.vector.tensor_scalar(out=cmat[:, 0:1], in0=dm[:], scalar1=rstd[:, 0:1], scalar2=None, op0=ALU.mult)
        nc.vector.tensor_scalar(out=c32[:], in0=dm[:], scalar1=rstd[:, 0:1], scalar2=None, op0=ALU.mult)
        centre_times_gamma(*fill[3])
        nc.vector.tensor_tensor(out=cmat[:, 1:2], in0=c32[:], in1=cmat[:, 0:1], op=ALU.subtract)
        tp = paux.tile([P, P], BF16, name="tp", tag="aux")
        nc.tensor.transpose(tp[:], cmat[:], ident_b[:])
        nc.scalar.copy(out=lt[:], in_=tp[:])
        nc.vector.scalar_tensor_tensor(
            out=y_first[:], in0=gamma_bc[:, 0:256], scalar=c32[:, 0:1], in1=beta_first[:], op0=ALU.mult, op1=ALU.add
        )
        centre_times_gamma(*fill[4])
        nc.vector.scalar_tensor_tensor(
            out=hg[:, 0:256], in0=hg[:, 0:256], scalar=rstd[:, 0:1], in1=y_first[:], op0=ALU.mult, op1=ALU.add
        )
        nc.sync.dma_start(out=of[:, 0:256], in_=hg[:, 0:256])
        widths = (256,) + (512,) * (DO // 512 - 2) + (256, 256)
        for j, width in enumerate(widths):
            c0 = 256 + sum(widths[:j])
            cols = slice(c0, c0 + width)
            if j % 3 == 2:
                shift = paux.tile([P, width], F32, name="shift", tag="aux")
            else:
                shift = pacc.tile([P, width], F32, name="shift", tag="acc")
            nc.tensor.matmul(out=shift[:], lhsT=lt[:], rhs=vmat[:, cols], start=True, stop=True)
            nc.vector.scalar_tensor_tensor(
                out=hg[:, cols], in0=hg[:, cols], scalar=rstd[:, 0:1], in1=shift[:], op0=ALU.mult, op1=ALU.add
            )
            nc.sync.dma_start(out=of[:, cols], in_=hg[:, cols])
